import numpy as np
import ml_dtypes


def mxq(x, axis, fmt="e4m3"):
    dtype, down = {"e4m3": (ml_dtypes.float8_e4m3fn, 7), "e5m2": (ml_dtypes.float8_e5m2, 14)}[fmt]
    v = np.moveaxis(np.asarray(x, np.float32).astype(ml_dtypes.bfloat16).astype(np.float64), axis, -1)
    blocks = v.reshape(v.shape[:-1] + (-1, 32))
    amax = np.abs(blocks).max(-1, keepdims=True)
    byte = np.maximum(np.where(amax > 0, np.frexp(amax)[1] - 1 + 127, 0) - down, 1)
    scale = np.exp2(byte - 127.0)
    codes = (blocks / scale).astype(np.float32).astype(dtype).astype(np.float64)
    return np.moveaxis((codes * scale).reshape(v.shape), -1, axis)


WIDE = False


def mx_kscale(k):
    if not WIDE:
        return np.ones(k)
    levels = np.array([10, -10, 5, -5, 0])
    a = np.random.permutation(np.resize(levels, k // 512 * 4)).reshape(k // 512, 4)
    idx = np.arange(k)
    return np.exp2(a[idx // 512, idx % 128 // 32])


BF16 = ml_dtypes.bfloat16


def bf(x):
    return np.asarray(x, np.float32).astype(BF16)


def f64(x):
    return np.asarray(x).astype(np.float64)


E2M1 = np.array([0.0, 0.5, 1.0, 1.5, 2.0, 3.0, 4.0, 6.0, -0.0, -0.5, -1.0, -1.5, -2.0, -3.0, -4.0, -6.0])


def pack_weight(w, fmt):
    k, n = w.shape
    w = f64(bf(w)).reshape(k // 32, 32, n)
    amax = np.abs(w).max(1)
    if fmt == "e4m3":
        byte = np.frexp(amax)[1] - 1 + 127 - 7
    else:
        mant, ex = np.frexp(amax / 6.0)
        byte = np.where(mant > 0.5, ex, ex - 1) + 127
    byte = np.clip(np.where(amax > 0, byte, 1), 1, 254)
    scaled = (w * np.exp2(127.0 - byte)[:, None, :]).reshape(k, n).astype(np.float32)
    by_word = np.ascontiguousarray(scaled.reshape(k // 512, 128, 4, n).transpose(0, 1, 3, 2))
    if fmt == "e4m3":
        words = by_word.astype(ml_dtypes.float8_e4m3fn).view(np.uint8)
    else:
        c = by_word.astype(ml_dtypes.float4_e2m1fn).view(np.uint8) & 0xF
        words = c[..., 0::2] | (c[..., 1::2] << 4)
    return np.ascontiguousarray(words), np.ascontiguousarray(byte.astype(np.uint8).reshape(k // 512, 16, n))


def unpack_weight(words, scales, fmt):
    g, p, n, _ = words.shape
    if fmt == "e4m3":
        vals = np.ascontiguousarray(words).view(ml_dtypes.float8_e4m3fn).astype(np.float64)
    else:
        nib = np.empty((g, p, n, 4), np.uint8)
        nib[..., 0::2] = words & 0xF
        nib[..., 1::2] = words >> 4
        vals = E2M1[nib]
    vals = vals * np.repeat(np.exp2(scales.astype(np.float64) - 127.0), 8, axis=1)[..., None]
    return vals.transpose(0, 1, 3, 2).reshape(g * 512, n)


B, N, F_IN, D_OUT, EMB_DIM, H1 = 1, 2048, 512, 128, 16, 4
NEG_INF = -1e9
LN_EPS = 1e-3


def setup_inputs():
    r = np.random.standard_normal
    s = mx_kscale(F_IN)
    adj = (0.3 + 0.4 * np.random.random_sample((N, N))) * (np.random.random_sample((N, N)) < 0.5)
    np.fill_diagonal(adj, 1.0)
    q2 = bf(r((B, N, D_OUT)) * 1.6)
    k2 = bf(r((B, N, D_OUT)) * 1.6)
    v2 = bf(r((B, N, D_OUT)) * 0.2)
    adj = bf(adj)
    x = bf(r((B, N, F_IN)) * s)
    proj_w_words, proj_w_scales = pack_weight(r((F_IN, D_OUT)) * 0.1 / np.sqrt(F_IN) / s[:, None], "e4m3")
    ln_g = bf(1.0 + 0.1 * r(D_OUT))
    ln_b = bf(0.1 * r(D_OUT))
    return {"q2": q2, "k2": k2, "v2": v2,
            "adj": adj,
            "x": x, "proj_w_words": proj_w_words, "proj_w_scales": proj_w_scales,
            "ln_g": ln_g, "ln_b": ln_b}


def reference(q2, k2, v2, adj, x, proj_w_words, proj_w_scales, ln_g, ln_b):
    scores = f64(q2) @ f64(k2).transpose(0, 2, 1) / np.sqrt(D_OUT)
    scores = np.where(f64(adj)[None] == 0, NEG_INF, scores)
    e = np.exp(scores - scores.max(-1, keepdims=True))
    h = (mxq(e, 2, "e4m3") @ mxq(f64(v2), 1, "e4m3")) / e.sum(-1, keepdims=True)
    skip = mxq(f64(x), 2, "e4m3") @ unpack_weight(proj_w_words, proj_w_scales, "e4m3")
    y = h + skip
    mu = y.mean(-1, keepdims=True)
    var = ((y - mu) ** 2).mean(-1, keepdims=True)
    return (y - mu) / np.sqrt(var + LN_EPS) * f64(ln_g) + f64(ln_b)

@@ -1,0 +1,367 @@
+from contextlib import ExitStack
+
+import concourse.mybir as mybir
+from concourse.masks import make_identity
+
+F32 = mybir.dt.float32
+BF16 = mybir.dt.bfloat16
+I32 = mybir.dt.int32
+U32 = mybir.dt.uint32
+U8 = mybir.dt.uint8
+FP8X4 = mybir.dt.float8_e4m3fn_x4
+ALU = mybir.AluOpType
+ACT = mybir.ActivationFunctionType
+AXIS = mybir.AxisListType
+
+P = 128
+PACK = 4
+K_PASS = P * PACK
+NODES = 2048
+D = 128
+F_IN = 512
+BANK = 512
+ROW_TILES = NODES // P
+KEY_BANKS = NODES // BANK
+KEY_PASSES = NODES // K_PASS
+QUAD = 4
+QUADS = ROW_TILES // QUAD
+LN_EPS = 1e-3
+
+MASK_SHIFT = 2.0 ** -34
+EXP_SCALE = 2.0 ** 34 / 128.0 ** 0.5
+
+FLOPS = 2 * NODES * NODES * D * 2 + 2 * NODES * F_IN * D
+
+
+def tile_spatialprocessor_pa_kernel(
+    tc, q2, k2, v2, adj, x, proj_w_words, proj_w_scales, ln_g, ln_b, out
+):
+    nc = tc.nc
+    with ExitStack() as pools:
+        keep = pools.enter_context(tc.tile_pool(name="keep", bufs=1))
+        adj_pool = pools.enter_context(tc.tile_pool(name="adj", bufs=ROW_TILES))
+        x_pool = pools.enter_context(tc.tile_pool(name="x", bufs=QUADS))
+        work = pools.enter_context(tc.tile_pool(name="work", bufs=3))
+        small = pools.enter_context(tc.tile_pool(name="small", bufs=4))
+        psum = pools.enter_context(tc.psum_pool(name="psum", bufs=1))
+        pools.enter_context(tc.manual_schedule())
+
+        k_rows = k2[0].rearrange("(c p m) d -> c p m d", p=P, m=PACK)
+        v_rows = v2[0].rearrange("(g p t) d -> p g t d", p=P, t=PACK)
+        q_rows = q2[0].rearrange("(p n) d -> p n d", n=ROW_TILES)
+        adj_rows = adj.rearrange("(p n) j -> p n j", n=ROW_TILES)
+        x_rows = x[0].rearrange("(p n) k -> p n k", n=ROW_TILES)
+        out_rows = out[0].rearrange("(p n) d -> p n d", n=ROW_TILES)
+
+        k_raw = keep.tile([P, KEY_BANKS, PACK, D], BF16)
+        q_raw = keep.tile([P, ROW_TILES, D], BF16)
+        v_raw = keep.tile([P, KEY_PASSES, PACK, D], BF16)
+        kT = keep.tile([P, NODES], BF16)
+        qT = keep.tile([P, ROW_TILES * P], BF16)
+        v_grouped = keep.tile([P, KEY_PASSES, D, PACK], BF16, align_bytes=64)
+        v_codes = keep.tile([P, KEY_PASSES * D], U32, align_bytes=64)
+        v_scales = keep.tile([P, KEY_PASSES * D], U8, align_bytes=64)
+        w_codes = keep.tile([P, D], U32, align_bytes=64)
+        w_scales = keep.tile([P, D], U8, align_bytes=64)
+        x_codes = keep.tile([P, ROW_TILES * P], U32, align_bytes=64)
+        x_scales = keep.tile([P, ROW_TILES * P], U8, align_bytes=64)
+        skip = keep.tile([P, ROW_TILES, D], F32)
+        gain = keep.tile([P, D], BF16)
+        shift = keep.tile([P, D], BF16)
+        ident_bf = keep.tile([P, P], BF16)
+        ident_f32 = keep.tile([P, P], F32)
+        minus_one = keep.tile([P, 1], F32)
+        minus_half = keep.tile([P, 1], F32)
+        adj_sb = [adj_pool.tile([P, NODES], BF16, name="adj_sb") for n in range(ROW_TILES)]
+        x_sb = [x_pool.tile([P, QUAD, F_IN], BF16, name="x_sb") for c in range(QUADS)]
+
+        s_ps = {}
+        t = {}
+        t_min = {}
+        e_words = {}
+        row_inv = {}
+        grouped = {}
+        x_grouped = {}
+        h_ps = {}
+        y = {}
+        neg_mean = {}
+
+        make_identity(nc, ident_bf[:])
+        make_identity(nc, ident_f32[:])
+        nc.gpsimd.memset(minus_one[:], -1.0)
+        nc.gpsimd.memset(minus_half[:], -0.5)
+        nc.vector.memset(w_scales[:].bitcast(I32), 0)
+
+        def load_keys(c):
+            nc.sync.dma_start(out=k_raw[:, c], in_=k_rows[c])
+
+        def load_queries(c):
+            tiles = slice(QUAD * c, QUAD * (c + 1))
+            nc.sync.dma_start(out=q_raw[:, tiles, :], in_=q_rows[:, tiles, :])
+
+        def load_adjacency(n):
+            nc.sync.dma_start(out=adj_sb[n][:], in_=adj_rows[:, n, :])
+
+        load_keys(0)
+        load_queries(0)
+        load_adjacency(0)
+        for c in range(1, KEY_BANKS):
+            load_keys(c)
+        load_adjacency(1)
+        nc.sync.dma_start(out=v_raw[:], in_=v_rows)
+        for c in range(1, QUADS):
+            load_queries(c)
+        nc.sync.dma_start(
+            out=w_codes[:].bitcast(I32),
+            in_=proj_w_words[0].rearrange("p n t -> p (n t)").bitcast(I32),
+        )
+        for quadrant in range(4):
+            nc.sync.dma_start(
+                out=w_scales[32 * quadrant : 32 * quadrant + 4, :].bitcast(I32),
+                in_=proj_w_scales[0, 4 * quadrant : 4 * quadrant + 4, :].bitcast(I32),
+            )
+        for c in range(QUADS):
+            nc.sync.dma_start(out=x_sb[c][:], in_=x_rows[:, QUAD * c : QUAD * (c + 1), :])
+            if c == 0:
+                nc.sync.dma_start(out=gain[:], in_=ln_g.partition_broadcast(P))
+                nc.sync.dma_start(out=shift[:], in_=ln_b.partition_broadcast(P))
+            for n in range(max(2, QUAD * c + 1), min(ROW_TILES, QUAD * c + 5)):
+                load_adjacency(n)
+
+        def transpose_keys(c):
+            kT_ps = psum.tile([P, PACK, P], BF16, tag="eT", bufs=2)
+            for m in range(PACK):
+                nc.tensor.transpose(kT_ps[:, m, :], k_raw[:, c, m, :], ident_bf[:])
+            nc.scalar.mul(
+                out=kT[:, BANK * c : BANK * (c + 1)].rearrange("d (p m) -> d p m", m=PACK),
+                in_=kT_ps[:].rearrange("d m p -> d p m"),
+                mul=MASK_SHIFT,
+            )
+
+        def transpose_queries(c):
+            qT_ps = psum.tile([P, QUAD * P], BF16, tag="eT", bufs=2)
+            for m in range(QUAD):
+                nc.tensor.transpose(
+                    qT_ps[:, P * m : P * (m + 1)], q_raw[:, QUAD * c + m, :], ident_bf[:]
+                )
+            nc.scalar.copy(out=qT[:, QUAD * P * c : QUAD * P * (c + 1)], in_=qT_ps[:])
+
+        def regroup_values():
+            nc.scalar.copy(out=v_grouped[:], in_=v_raw[:].rearrange("p g t d -> p g d t"))
+
+        def quantise_values():
+            nc.vector.quantize_mx(
+                out=v_codes[:].bitcast(FP8X4),
+                scales=v_scales[:],
+                in_=v_grouped[:].rearrange("p g d t -> p (g d t)"),
+            )
+
+        def skip_regroup(c):
+            x_words = x_sb[c][:].bitcast(F32)
+            x_grouped[c] = work.tile([P, QUAD, P, PACK], BF16, name="x_grouped", align_bytes=64)
+            x_grouped_words = x_grouped[c][:].bitcast(F32)
+            for half in range(2):
+                xT_ps = psum.tile([P, 2, 2, P], F32, tag="eT", bufs=2)
+                for m in range(2):
+                    for u in range(2):
+                        nc.tensor.transpose(
+                            xT_ps[:, m, u, :], x_words[:, 2 * half + m, u : F_IN // 2 : 2], ident_f32[:]
+                        )
+                nc.scalar.copy(
+                    out=x_grouped_words[:, 2 * half : 2 * half + 2, :, :],
+                    in_=xT_ps[:].rearrange("p m u i -> p m i u"),
+                )
+
+        def skip_product(c):
+            cols = slice(QUAD * P * c, QUAD * P * (c + 1))
+            nc.vector.quantize_mx(
+                out=x_codes[:, cols].bitcast(FP8X4),
+                scales=x_scales[:, cols],
+                in_=x_grouped[c][:].rearrange("p m i t -> p (m i t)"),
+            )
+            skip_ps = psum.tile([P, QUAD, D], F32, tag="skip", bufs=1)
+            for m in range(QUAD):
+                nodes = slice(P * (QUAD * c + m), P * (QUAD * c + m + 1))
+                nc.tensor.matmul_mx(
+                    out=skip_ps[:, m, :],
+                    lhsT=x_codes[:, nodes].bitcast(FP8X4),
+                    lhsT_scale=x_scales[:, nodes],
+                    rhs=w_codes[:].bitcast(FP8X4),
+                    rhs_scale=w_scales[:],
+                    start=True,
+                    stop=True,
+                )
+            nc.scalar.copy(out=skip[:, QUAD * c : QUAD * (c + 1), :], in_=skip_ps[:])
+
+        def scores(n, half):
+            for b in range(2 * half, 2 * half + 2):
+                s_ps[n, b] = psum.tile([P, BANK], F32, name="s_ps", tag="s", bufs=KEY_BANKS)
+                nc.tensor.matmul(
+                    out=s_ps[n, b][:],
+                    lhsT=qT[:, P * n : P * (n + 1)],
+                    rhs=kT[:, BANK * b : BANK * (b + 1)],
+                    start=True,
+                    stop=True,
+                )
+
+        def mask_scores(n, half):
+            if half == 0:
+                t[n] = work.tile([P, NODES], F32, name="t")
+            for b in range(2 * half, 2 * half + 2):
+                keys = slice(BANK * b, BANK * (b + 1))
+                nc.vector.scalar_tensor_tensor(
+                    out=t[n][:, keys],
+                    in0=adj_sb[n][:, keys],
+                    scalar=0.0,
+                    in1=s_ps[n, b][:],
+                    op0=ALU.is_equal,
+                    op1=ALU.subtract,
+                )
+
+        def row_minimum(n):
+            t_min[n] = small.tile([P, 1], F32, name="t_min")
+            nc.vector.tensor_reduce(out=t_min[n][:], in_=t[n][:], axis=AXIS.X, op=ALU.min)
+
+        def exponentials(n):
+            exp_bias = small.tile([P, 1], F32)
+            nc.scalar.mul(out=exp_bias[:], in_=t_min[n][:], mul=EXP_SCALE)
+            e_sb = work.tile([P, NODES], BF16)
+            e_words[n] = e_sb[:].bitcast(F32)
+            row_sums = small.tile([P, 2], F32)
+            for half in range(2):
+                keys = slice(NODES // 2 * half, NODES // 2 * (half + 1))
+                nc.scalar.activation(
+                    out=e_sb[:, keys].rearrange("i (u w e) -> i u w e", u=2, e=2),
+                    in_=t[n][:, keys].rearrange("i (w u e) -> i u w e", u=2, e=2),
+                    func=ACT.Exp,
+                    bias=exp_bias[:, 0:1],
+                    scale=-EXP_SCALE,
+                    accum_out=row_sums[:, half : half + 1],
+                )
+            row_sum = small.tile([P, 1], F32)
+            nc.gpsimd.tensor_tensor(out=row_sum[:], in0=row_sums[:, 0:1], in1=row_sums[:, 1:2], op=ALU.add)
+            row_inv[n] = small.tile([P, 1], F32, name="row_inv")
+            nc.gpsimd.tensor_tensor(out=row_inv[n][:], in0=row_sum[:], in1=minus_one[:], op=ALU.pow)
+
+        def regroup(n, half):
+            if half == 0:
+                grouped[n] = work.tile([P, KEY_PASSES, P, PACK], BF16, name="grouped", align_bytes=64)
+            grouped_words = grouped[n][:].bitcast(F32)
+            eT_ps = psum.tile([P, 2, 2, P], F32, tag="eT", bufs=2)
+            for g in range(2):
+                for u in range(2):
+                    first = P * (4 * half + 2 * u + g)
+                    nc.tensor.transpose(eT_ps[:, g, u, :], e_words[n][:, first : first + P], ident_f32[:])
+            nc.scalar.copy(
+                out=grouped_words[:, 2 * half : 2 * half + 2, :, :],
+                in_=eT_ps[:].rearrange("p g u i -> p g i u"),
+            )
+
+        def weighted_values(n):
+            e_codes = work.tile([P, KEY_PASSES * P], U32, align_bytes=64)
+            e_scales = work.tile([P, KEY_PASSES * P], U8, align_bytes=64)
+            nc.vector.quantize_mx(
+                out=e_codes[:].bitcast(FP8X4),
+                scales=e_scales[:],
+                in_=grouped[n][:].rearrange("p g i t -> p (g i t)"),
+            )
+            h_ps[n] = psum.tile([P, D], F32, name="h_ps", tag="h", bufs=1)
+            for g in range(KEY_PASSES):
+                cols = slice(P * g, P * (g + 1))
+                nc.tensor.matmul_mx(
+                    out=h_ps[n][:],
+                    lhsT=e_codes[:, cols].bitcast(FP8X4),
+                    lhsT_scale=e_scales[:, cols],
+                    rhs=v_codes[:, cols].bitcast(FP8X4),
+                    rhs_scale=v_scales[:, cols],
+                    start=(g == 0),
+                    stop=(g == KEY_PASSES - 1),
+                )
+
+        def add_streams(n):
+            y[n] = work.tile([P, D], F32, name="y")
+            y_sum = small.tile([P, 1], F32)
+            nc.vector.scalar_tensor_tensor(
+                out=y[n][:],
+                in0=h_ps[n][:],
+                scalar=row_inv[n][:, 0:1],
+                in1=skip[:, n, :],
+                op0=ALU.mult,
+                op1=ALU.add,
+                accum_out=y_sum[:],
+            )
+            neg_mean[n] = small.tile([P, 1], F32, name="neg_mean")
+            nc.gpsimd.tensor_scalar(
+                out=neg_mean[n][:], in0=y_sum[:], scalar1=-1.0 / D, scalar2=0.0, op0=ALU.mult, op1=ALU.add
+            )
+
+        def layer_norm(n):
+            squares = work.tile([P, D], F32)
+            sq_sum = small.tile([P, 1], F32)
+            nc.scalar.activation(
+                out=squares[:],
+                in_=y[n][:],
+                func=ACT.Square,
+                bias=neg_mean[n][:, 0:1],
+                scale=1.0,
+                accum_out=sq_sum[:],
+            )
+            var_eps = small.tile([P, 1], F32)
+            nc.gpsimd.tensor_scalar(
+                out=var_eps[:], in0=sq_sum[:], scalar1=1.0 / D, scalar2=LN_EPS, op0=ALU.mult, op1=ALU.add
+            )
+            inv_std = small.tile([P, 1], F32)
+            nc.gpsimd.tensor_tensor(out=inv_std[:], in0=var_eps[:], in1=minus_half[:], op=ALU.pow)
+            normed = work.tile([P, D], F32)
+            nc.gpsimd.tensor_scalar(
+                out=normed[:],
+                in0=y[n][:],
+                scalar1=neg_mean[n][:, 0:1],
+                scalar2=inv_std[:, 0:1],
+                op0=ALU.add,
+                op1=ALU.mult,
+            )
+            scaled = work.tile([P, D], F32)
+            nc.gpsimd.tensor_tensor(out=scaled[:], in0=normed[:], in1=gain[:], op=ALU.mult)
+            result = work.tile([P, D], F32)
+            nc.gpsimd.tensor_tensor(out=result[:], in0=scaled[:], in1=shift[:], op=ALU.add)
+            nc.sync.dma_start(out=out_rows[:, n, :], in_=result[:])
+
+        def is_tile(n):
+            return 0 <= n < ROW_TILES
+
+        transpose_keys(0)
+        transpose_queries(0)
+        transpose_keys(1)
+        scores(0, 0)
+        transpose_keys(2)
+        transpose_keys(3)
+        scores(0, 1)
+
+        for step in range(ROW_TILES + 3):
+            if is_tile(step - 1):
+                exponentials(step - 1)
+            for half in range(2):
+                if is_tile(step):
+                    mask_scores(step, half)
+                if is_tile(step + 1):
+                    scores(step + 1, half)
+                if is_tile(step - 1):
+                    regroup(step - 1, half)
+            if is_tile(step - 2):
+                weighted_values(step - 2)
+            if is_tile(step) and step % QUAD == 1:
+                skip_product(step // QUAD)
+            if is_tile(step):
+                row_minimum(step)
+            if is_tile(step - 2):
+                add_streams(step - 2)
+            if is_tile(step - 3):
+                layer_norm(step - 3)
+            if step == 0:
+                regroup_values()
+                for c in range(1, QUADS):
+                    transpose_queries(c)
+                quantise_values()
+            if is_tile(step) and step % QUAD == 0:
+                skip_regroup(step // QUAD)

@@ -81,10 +81,14 @@ def tile_spatialprocessor_pa_kernel(
         e_words = {}
         row_inv = {}
         grouped = {}
+        xT_ps = {}
         x_grouped = {}
+        skip_ps = {}
+        e_codes = {}
+        e_scales = {}
+        y_sum = {}
         h_ps = {}
         y = {}
-        neg_mean = {}
 
         make_identity(nc, ident_bf[:])
         make_identity(nc, ident_f32[:])
@@ -99,6 +103,9 @@ def tile_spatialprocessor_pa_kernel(
             tiles = slice(QUAD * c, QUAD * (c + 1))
             nc.sync.dma_start(out=q_raw[:, tiles, :], in_=q_rows[:, tiles, :])
 
+        def load_features(c):
+            nc.sync.dma_start(out=x_sb[c][:], in_=x_rows[:, QUAD * c : QUAD * (c + 1), :])
+
         def load_adjacency(n):
             nc.sync.dma_start(out=adj_sb[n][:], in_=adj_rows[:, n, :])
 
@@ -107,10 +114,11 @@ def tile_spatialprocessor_pa_kernel(
         load_adjacency(0)
         for c in range(1, KEY_BANKS):
             load_keys(c)
-        load_adjacency(1)
         nc.sync.dma_start(out=v_raw[:], in_=v_rows)
         for c in range(1, QUADS):
             load_queries(c)
+        load_adjacency(1)
+        load_features(0)
         nc.sync.dma_start(
             out=w_codes[:].bitcast(I32),
             in_=proj_w_words[0].rearrange("p n t -> p (n t)").bitcast(I32),
@@ -120,13 +128,12 @@ def tile_spatialprocessor_pa_kernel(
                 out=w_scales[32 * quadrant : 32 * quadrant + 4, :].bitcast(I32),
                 in_=proj_w_scales[0, 4 * quadrant : 4 * quadrant + 4, :].bitcast(I32),
             )
-        for c in range(QUADS):
-            nc.sync.dma_start(out=x_sb[c][:], in_=x_rows[:, QUAD * c : QUAD * (c + 1), :])
-            if c == 0:
-                nc.sync.dma_start(out=gain[:], in_=ln_g.partition_broadcast(P))
-                nc.sync.dma_start(out=shift[:], in_=ln_b.partition_broadcast(P))
-            for n in range(max(2, QUAD * c + 1), min(ROW_TILES, QUAD * c + 5)):
-                load_adjacency(n)
+        nc.sync.dma_start(out=gain[:], in_=ln_g.partition_broadcast(P))
+        nc.sync.dma_start(out=shift[:], in_=ln_b.partition_broadcast(P))
+        for n in range(2, ROW_TILES):
+            load_adjacency(n)
+            if n % QUAD == 2 and n // QUAD + 1 < QUADS:
+                load_features(n // QUAD + 1)
 
         def transpose_keys(c):
             kT_ps = psum.tile([P, PACK, P], BF16, tag="eT", bufs=2)
@@ -156,21 +163,23 @@ def tile_spatialprocessor_pa_kernel(
                 in_=v_grouped[:].rearrange("p g d t -> p (g d t)"),
             )
 
-        def skip_regroup(c):
+        def transpose_features(c, half):
             x_words = x_sb[c][:].bitcast(F32)
-            x_grouped[c] = work.tile([P, QUAD, P, PACK], BF16, name="x_grouped", align_bytes=64)
+            xT_ps[c, half] = psum.tile([P, 2, 2, P], F32, name="xT_ps", tag="side", bufs=1)
+            for m in range(2):
+                for u in range(2):
+                    nc.tensor.transpose(
+                        xT_ps[c, half][:, m, u, :], x_words[:, 2 * half + m, u : F_IN // 2 : 2], ident_f32[:]
+                    )
+
+        def regroup_features(c, half):
+            if half == 0:
+                x_grouped[c] = work.tile([P, QUAD, P, PACK], BF16, name="x_grouped", align_bytes=64)
             x_grouped_words = x_grouped[c][:].bitcast(F32)
-            for half in range(2):
-                xT_ps = psum.tile([P, 2, 2, P], F32, tag="eT", bufs=2)
-                for m in range(2):
-                    for u in range(2):
-                        nc.tensor.transpose(
-                            xT_ps[:, m, u, :], x_words[:, 2 * half + m, u : F_IN // 2 : 2], ident_f32[:]
-                        )
-                nc.scalar.copy(
-                    out=x_grouped_words[:, 2 * half : 2 * half + 2, :, :],
-                    in_=xT_ps[:].rearrange("p m u i -> p m i u"),
-                )
+            nc.scalar.copy(
+                out=x_grouped_words[:, 2 * half : 2 * half + 2, :, :],
+                in_=xT_ps[c, half][:].rearrange("p m u i -> p m i u"),
+            )
 
         def skip_product(c):
             cols = slice(QUAD * P * c, QUAD * P * (c + 1))
@@ -179,11 +188,11 @@ def tile_spatialprocessor_pa_kernel(
                 scales=x_scales[:, cols],
                 in_=x_grouped[c][:].rearrange("p m i t -> p (m i t)"),
             )
-            skip_ps = psum.tile([P, QUAD, D], F32, tag="skip", bufs=1)
+            skip_ps[c] = psum.tile([P, QUAD, D], F32, name="skip_ps", tag="side", bufs=1)
             for m in range(QUAD):
                 nodes = slice(P * (QUAD * c + m), P * (QUAD * c + m + 1))
                 nc.tensor.matmul_mx(
-                    out=skip_ps[:, m, :],
+                    out=skip_ps[c][:, m, :],
                     lhsT=x_codes[:, nodes].bitcast(FP8X4),
                     lhsT_scale=x_scales[:, nodes],
                     rhs=w_codes[:].bitcast(FP8X4),
@@ -191,32 +200,32 @@ def tile_spatialprocessor_pa_kernel(
                     start=True,
                     stop=True,
                 )
-            nc.scalar.copy(out=skip[:, QUAD * c : QUAD * (c + 1), :], in_=skip_ps[:])
 
-        def scores(n, half):
-            for b in range(2 * half, 2 * half + 2):
-                s_ps[n, b] = psum.tile([P, BANK], F32, name="s_ps", tag="s", bufs=KEY_BANKS)
-                nc.tensor.matmul(
-                    out=s_ps[n, b][:],
-                    lhsT=qT[:, P * n : P * (n + 1)],
-                    rhs=kT[:, BANK * b : BANK * (b + 1)],
-                    start=True,
-                    stop=True,
-                )
+        def keep_skip(c):
+            nc.scalar.copy(out=skip[:, QUAD * c : QUAD * (c + 1), :], in_=skip_ps[c][:])
 
-        def mask_scores(n, half):
-            if half == 0:
+        def scores(n, b):
+            s_ps[n, b] = psum.tile([P, BANK], F32, name="s_ps", tag="s", bufs=KEY_BANKS)
+            nc.tensor.matmul(
+                out=s_ps[n, b][:],
+                lhsT=qT[:, P * n : P * (n + 1)],
+                rhs=kT[:, BANK * b : BANK * (b + 1)],
+                start=True,
+                stop=True,
+            )
+
+        def mask_scores(n, b):
+            if b == 0:
                 t[n] = work.tile([P, NODES], F32, name="t")
-            for b in range(2 * half, 2 * half + 2):
-                keys = slice(BANK * b, BANK * (b + 1))
-                nc.vector.scalar_tensor_tensor(
-                    out=t[n][:, keys],
-                    in0=adj_sb[n][:, keys],
-                    scalar=0.0,
-                    in1=s_ps[n, b][:],
-                    op0=ALU.is_equal,
-                    op1=ALU.subtract,
-                )
+            keys = slice(BANK * b, BANK * (b + 1))
+            nc.vector.scalar_tensor_tensor(
+                out=t[n][:, keys],
+                in0=adj_sb[n][:, keys],
+                scalar=0.0,
+                in1=s_ps[n, b][:],
+                op0=ALU.is_equal,
+                op1=ALU.subtract,
+            )
 
         def row_minimum(n):
             t_min[n] = small.tile([P, 1], F32, name="t_min")
@@ -257,21 +266,25 @@ def tile_spatialprocessor_pa_kernel(
                 in_=eT_ps[:].rearrange("p g u i -> p g i u"),
             )
 
-        def weighted_values(n):
-            e_codes = work.tile([P, KEY_PASSES * P], U32, align_bytes=64)
-            e_scales = work.tile([P, KEY_PASSES * P], U8, align_bytes=64)
-            nc.vector.quantize_mx(
-                out=e_codes[:].bitcast(FP8X4),
-                scales=e_scales[:],
-                in_=grouped[n][:].rearrange("p g i t -> p (g i t)"),
-            )
+        def quantise_e(n):
+            e_codes[n] = work.tile([P, KEY_PASSES * P], U32, name="e_codes", align_bytes=64)
+            e_scales[n] = work.tile([P, KEY_PASSES * P], U8, name="e_scales", align_bytes=64)
+            for half in range(2):
+                cols = slice(2 * P * half, 2 * P * (half + 1))
+                nc.vector.quantize_mx(
+                    out=e_codes[n][:, cols].bitcast(FP8X4),
+                    scales=e_scales[n][:, cols],
+                    in_=grouped[n][:, 2 * half : 2 * half + 2].rearrange("p g i t -> p (g i t)"),
+                )
+
+        def multiply_values(n):
             h_ps[n] = psum.tile([P, D], F32, name="h_ps", tag="h", bufs=1)
             for g in range(KEY_PASSES):
                 cols = slice(P * g, P * (g + 1))
                 nc.tensor.matmul_mx(
                     out=h_ps[n][:],
-                    lhsT=e_codes[:, cols].bitcast(FP8X4),
-                    lhsT_scale=e_scales[:, cols],
+                    lhsT=e_codes[n][:, cols].bitcast(FP8X4),
+                    lhsT_scale=e_scales[n][:, cols],
                     rhs=v_codes[:, cols].bitcast(FP8X4),
                     rhs_scale=v_scales[:, cols],
                     start=(g == 0),
@@ -280,7 +293,7 @@ def tile_spatialprocessor_pa_kernel(
 
         def add_streams(n):
             y[n] = work.tile([P, D], F32, name="y")
-            y_sum = small.tile([P, 1], F32)
+            y_sum[n] = small.tile([P, 1], F32, name="y_sum")
             nc.vector.scalar_tensor_tensor(
                 out=y[n][:],
                 in0=h_ps[n][:],
@@ -288,80 +301,92 @@ def tile_spatialprocessor_pa_kernel(
                 in1=skip[:, n, :],
                 op0=ALU.mult,
                 op1=ALU.add,
-                accum_out=y_sum[:],
-            )
-            neg_mean[n] = small.tile([P, 1], F32, name="neg_mean")
-            nc.gpsimd.tensor_scalar(
-                out=neg_mean[n][:], in0=y_sum[:], scalar1=-1.0 / D, scalar2=0.0, op0=ALU.mult, op1=ALU.add
+                accum_out=y_sum[n][:],
             )
 
         def layer_norm(n):
+            elementwise = nc.vector if n == ROW_TILES - 1 else nc.gpsimd
+            neg_mean = small.tile([P, 1], F32)
+            nc.scalar.mul(out=neg_mean[:], in_=y_sum[n][:], mul=-1.0 / D)
             squares = work.tile([P, D], F32)
             sq_sum = small.tile([P, 1], F32)
             nc.scalar.activation(
                 out=squares[:],
                 in_=y[n][:],
                 func=ACT.Square,
-                bias=neg_mean[n][:, 0:1],
+                bias=neg_mean[:, 0:1],
                 scale=1.0,
                 accum_out=sq_sum[:],
             )
             var_eps = small.tile([P, 1], F32)
-            nc.gpsimd.tensor_scalar(
-                out=var_eps[:], in0=sq_sum[:], scalar1=1.0 / D, scalar2=LN_EPS, op0=ALU.mult, op1=ALU.add
-            )
+            nc.scalar.activation(out=var_eps[:], in_=sq_sum[:], func=ACT.Copy, bias=LN_EPS, scale=1.0 / D)
             inv_std = small.tile([P, 1], F32)
             nc.gpsimd.tensor_tensor(out=inv_std[:], in0=var_eps[:], in1=minus_half[:], op=ALU.pow)
             normed = work.tile([P, D], F32)
-            nc.gpsimd.tensor_scalar(
+            elementwise.tensor_scalar(
                 out=normed[:],
                 in0=y[n][:],
-                scalar1=neg_mean[n][:, 0:1],
+                scalar1=neg_mean[:, 0:1],
                 scalar2=inv_std[:, 0:1],
                 op0=ALU.add,
                 op1=ALU.mult,
             )
             scaled = work.tile([P, D], F32)
-            nc.gpsimd.tensor_tensor(out=scaled[:], in0=normed[:], in1=gain[:], op=ALU.mult)
+            elementwise.tensor_tensor(out=scaled[:], in0=normed[:], in1=gain[:], op=ALU.mult)
             result = work.tile([P, D], F32)
-            nc.gpsimd.tensor_tensor(out=result[:], in0=scaled[:], in1=shift[:], op=ALU.add)
+            elementwise.tensor_tensor(out=result[:], in0=scaled[:], in1=shift[:], op=ALU.add)
             nc.sync.dma_start(out=out_rows[:, n, :], in_=result[:])
 
         def is_tile(n):
             return 0 <= n < ROW_TILES
 
+        def side_job_start(step):
+            quad, phase = divmod(step, QUAD)
+            if phase < 2:
+                transpose_features(quad, phase)
+            elif phase == 2:
+                skip_product(quad)
+
+        def side_job_finish(step):
+            quad, phase = divmod(step, QUAD)
+            if phase < 2:
+                regroup_features(quad, phase)
+            elif phase == 2:
+                keep_skip(quad)
+
         transpose_keys(0)
         transpose_queries(0)
-        transpose_keys(1)
         scores(0, 0)
-        transpose_keys(2)
-        transpose_keys(3)
-        scores(0, 1)
+        for b in range(1, KEY_BANKS):
+            transpose_keys(b)
+            scores(0, b)
+        regroup_values()
 
-        for step in range(ROW_TILES + 3):
+        for step in range(ROW_TILES + 4):
             if is_tile(step - 1):
                 exponentials(step - 1)
-            for half in range(2):
+                side_job_finish(step - 1)
+            for b in range(KEY_BANKS):
                 if is_tile(step):
-                    mask_scores(step, half)
+                    mask_scores(step, b)
                 if is_tile(step + 1):
-                    scores(step + 1, half)
-                if is_tile(step - 1):
-                    regroup(step - 1, half)
+                    scores(step + 1, b)
+                if is_tile(step - 1) and b < 2:
+                    regroup(step - 1, b)
+            if is_tile(step - 4):
+                layer_norm(step - 4)
+            if step == 1:
+                quantise_values()
             if is_tile(step - 2):
-                weighted_values(step - 2)
-            if is_tile(step) and step % QUAD == 1:
-                skip_product(step // QUAD)
+                quantise_e(step - 2)
             if is_tile(step):
                 row_minimum(step)
-            if is_tile(step - 2):
-                add_streams(step - 2)
             if is_tile(step - 3):
-                layer_norm(step - 3)
+                add_streams(step - 3)
+            if is_tile(step - 2):
+                multiply_values(step - 2)
             if step == 0:
-                regroup_values()
                 for c in range(1, QUADS):
                     transpose_queries(c)
-                quantise_values()
-            if is_tile(step) and step % QUAD == 0:
-                skip_regroup(step // QUAD)
+            if is_tile(step):
+                side_job_start(step)

@@ -26,6 +26,8 @@ KEY_PASSES = NODES // K_PASS
 QUAD = 4
 QUADS = ROW_TILES // QUAD
 LN_EPS = 1e-3
+TURN_BANKS = 3
+NORMALISE_LAG = 4
 
 MASK_SHIFT = 2.0 ** -34
 EXP_SCALE = 2.0 ** 34 / 128.0 ** 0.5
@@ -78,15 +80,19 @@ def tile_spatialprocessor_pa_kernel(
         s_ps = {}
         t = {}
         t_min = {}
+        exp_bias = {}
         e_words = {}
         row_inv = {}
         grouped = {}
+        qT_ps = {}
         xT_ps = {}
         x_grouped = {}
         skip_ps = {}
         e_codes = {}
         e_scales = {}
         y_sum = {}
+        neg_mean = {}
+        inv_std = {}
         h_ps = {}
         y = {}
 
@@ -111,14 +117,14 @@ def tile_spatialprocessor_pa_kernel(
 
         load_keys(0)
         load_queries(0)
-        load_adjacency(0)
         for c in range(1, KEY_BANKS):
             load_keys(c)
+        load_adjacency(0)
         nc.sync.dma_start(out=v_raw[:], in_=v_rows)
+        load_features(0)
+        load_adjacency(1)
         for c in range(1, QUADS):
             load_queries(c)
-        load_adjacency(1)
-        load_features(0)
         nc.sync.dma_start(
             out=w_codes[:].bitcast(I32),
             in_=proj_w_words[0].rearrange("p n t -> p (n t)").bitcast(I32),
@@ -136,7 +142,7 @@ def tile_spatialprocessor_pa_kernel(
                 load_features(n // QUAD + 1)
 
         def transpose_keys(c):
-            kT_ps = psum.tile([P, PACK, P], BF16, tag="eT", bufs=2)
+            kT_ps = psum.tile([P, PACK, P], BF16, tag="s", bufs=KEY_BANKS)
             for m in range(PACK):
                 nc.tensor.transpose(kT_ps[:, m, :], k_raw[:, c, m, :], ident_bf[:])
             nc.scalar.mul(
@@ -146,12 +152,14 @@ def tile_spatialprocessor_pa_kernel(
             )
 
         def transpose_queries(c):
-            qT_ps = psum.tile([P, QUAD * P], BF16, tag="eT", bufs=2)
+            qT_ps[c] = psum.tile([P, QUAD * P], BF16, name="qT_ps", tag="turn", bufs=TURN_BANKS)
             for m in range(QUAD):
                 nc.tensor.transpose(
-                    qT_ps[:, P * m : P * (m + 1)], q_raw[:, QUAD * c + m, :], ident_bf[:]
+                    qT_ps[c][:, P * m : P * (m + 1)], q_raw[:, QUAD * c + m, :], ident_bf[:]
                 )
-            nc.scalar.copy(out=qT[:, QUAD * P * c : QUAD * P * (c + 1)], in_=qT_ps[:])
+
+        def keep_queries(c):
+            nc.scalar.copy(out=qT[:, QUAD * P * c : QUAD * P * (c + 1)], in_=qT_ps[c][:])
 
         def regroup_values():
             nc.scalar.copy(out=v_grouped[:], in_=v_raw[:].rearrange("p g t d -> p g d t"))
@@ -165,7 +173,7 @@ def tile_spatialprocessor_pa_kernel(
 
         def transpose_features(c, half):
             x_words = x_sb[c][:].bitcast(F32)
-            xT_ps[c, half] = psum.tile([P, 2, 2, P], F32, name="xT_ps", tag="side", bufs=1)
+            xT_ps[c, half] = psum.tile([P, 2, 2, P], F32, name="xT_ps", tag="turn", bufs=TURN_BANKS)
             for m in range(2):
                 for u in range(2):
                     nc.tensor.transpose(
@@ -188,7 +196,7 @@ def tile_spatialprocessor_pa_kernel(
                 scales=x_scales[:, cols],
                 in_=x_grouped[c][:].rearrange("p m i t -> p (m i t)"),
             )
-            skip_ps[c] = psum.tile([P, QUAD, D], F32, name="skip_ps", tag="side", bufs=1)
+            skip_ps[c] = psum.tile([P, QUAD, D], F32, name="skip_ps", tag="turn", bufs=TURN_BANKS)
             for m in range(QUAD):
                 nodes = slice(P * (QUAD * c + m), P * (QUAD * c + m + 1))
                 nc.tensor.matmul_mx(
@@ -231,9 +239,11 @@ def tile_spatialprocessor_pa_kernel(
             t_min[n] = small.tile([P, 1], F32, name="t_min")
             nc.vector.tensor_reduce(out=t_min[n][:], in_=t[n][:], axis=AXIS.X, op=ALU.min)
 
+        def exponent_offset(n):
+            exp_bias[n] = small.tile([P, 1], F32, name="exp_bias")
+            nc.scalar.mul(out=exp_bias[n][:], in_=t_min[n][:], mul=EXP_SCALE)
+
         def exponentials(n):
-            exp_bias = small.tile([P, 1], F32)
-            nc.scalar.mul(out=exp_bias[:], in_=t_min[n][:], mul=EXP_SCALE)
             e_sb = work.tile([P, NODES], BF16)
             e_words[n] = e_sb[:].bitcast(F32)
             row_sums = small.tile([P, 2], F32)
@@ -243,7 +253,7 @@ def tile_spatialprocessor_pa_kernel(
                     out=e_sb[:, keys].rearrange("i (u w e) -> i u w e", u=2, e=2),
                     in_=t[n][:, keys].rearrange("i (w u e) -> i u w e", u=2, e=2),
                     func=ACT.Exp,
-                    bias=exp_bias[:, 0:1],
+                    bias=exp_bias[n][:, 0:1],
                     scale=-EXP_SCALE,
                     accum_out=row_sums[:, half : half + 1],
                 )
@@ -256,7 +266,7 @@ def tile_spatialprocessor_pa_kernel(
             if half == 0:
                 grouped[n] = work.tile([P, KEY_PASSES, P, PACK], BF16, name="grouped", align_bytes=64)
             grouped_words = grouped[n][:].bitcast(F32)
-            eT_ps = psum.tile([P, 2, 2, P], F32, tag="eT", bufs=2)
+            eT_ps = psum.tile([P, 2, 2, P], F32, tag="turn", bufs=TURN_BANKS)
             for g in range(2):
                 for u in range(2):
                     first = P * (4 * half + 2 * u + g)
@@ -304,30 +314,34 @@ def tile_spatialprocessor_pa_kernel(
                 accum_out=y_sum[n][:],
             )
 
-        def layer_norm(n):
-            elementwise = nc.vector if n == ROW_TILES - 1 else nc.gpsimd
-            neg_mean = small.tile([P, 1], F32)
-            nc.scalar.mul(out=neg_mean[:], in_=y_sum[n][:], mul=-1.0 / D)
+        def row_mean(n):
+            neg_mean[n] = small.tile([P, 1], F32, name="neg_mean")
+            nc.scalar.mul(out=neg_mean[n][:], in_=y_sum[n][:], mul=-1.0 / D)
+
+        def row_deviation(n):
             squares = work.tile([P, D], F32)
             sq_sum = small.tile([P, 1], F32)
             nc.scalar.activation(
                 out=squares[:],
                 in_=y[n][:],
                 func=ACT.Square,
-                bias=neg_mean[:, 0:1],
+                bias=neg_mean[n][:, 0:1],
                 scale=1.0,
                 accum_out=sq_sum[:],
             )
             var_eps = small.tile([P, 1], F32)
             nc.scalar.activation(out=var_eps[:], in_=sq_sum[:], func=ACT.Copy, bias=LN_EPS, scale=1.0 / D)
-            inv_std = small.tile([P, 1], F32)
-            nc.gpsimd.tensor_tensor(out=inv_std[:], in0=var_eps[:], in1=minus_half[:], op=ALU.pow)
+            inv_std[n] = small.tile([P, 1], F32, name="inv_std")
+            nc.gpsimd.tensor_tensor(out=inv_std[n][:], in0=var_eps[:], in1=minus_half[:], op=ALU.pow)
+
+        def normalise(n):
+            elementwise = nc.vector if n + NORMALISE_LAG >= ROW_TILES else nc.gpsimd
             normed = work.tile([P, D], F32)
             elementwise.tensor_scalar(
                 out=normed[:],
                 in0=y[n][:],
-                scalar1=neg_mean[:, 0:1],
-                scalar2=inv_std[:, 0:1],
+                scalar1=neg_mean[n][:, 0:1],
+                scalar2=inv_std[n][:, 0:1],
                 op0=ALU.add,
                 op1=ALU.mult,
             )
@@ -340,32 +354,50 @@ def tile_spatialprocessor_pa_kernel(
         def is_tile(n):
             return 0 <= n < ROW_TILES
 
-        def side_job_start(step):
-            quad, phase = divmod(step, QUAD)
+        def side_job_start(k):
+            quad, phase = divmod(k, QUAD)
             if phase < 2:
                 transpose_features(quad, phase)
             elif phase == 2:
                 skip_product(quad)
+            elif quad + 1 < QUADS:
+                transpose_queries(quad + 1)
 
-        def side_job_finish(step):
-            quad, phase = divmod(step, QUAD)
+        def side_job_finish(k):
+            quad, phase = divmod(k, QUAD)
             if phase < 2:
                 regroup_features(quad, phase)
             elif phase == 2:
                 keep_skip(quad)
+            elif quad + 1 < QUADS:
+                keep_queries(quad + 1)
 
         transpose_keys(0)
         transpose_queries(0)
-        scores(0, 0)
-        for b in range(1, KEY_BANKS):
-            transpose_keys(b)
+        keep_queries(0)
+        for c in range(1, KEY_BANKS):
+            transpose_keys(c)
+        for b in range(KEY_BANKS):
             scores(0, b)
         regroup_values()
+        side_job_start(0)
+        side_job_start(1)
+        side_job_finish(0)
 
-        for step in range(ROW_TILES + 4):
+        for step in range(ROW_TILES + NORMALISE_LAG):
+            if is_tile(step - 1):
+                exponent_offset(step - 1)
+            if is_tile(step - 3):
+                row_mean(step - 3)
             if is_tile(step - 1):
                 exponentials(step - 1)
-                side_job_finish(step - 1)
+            if is_tile(step + 1):
+                side_job_finish(step + 1)
+            if step == 1:
+                quantise_values()
+            if is_tile(step - 2):
+                quantise_e(step - 2)
+                multiply_values(step - 2)
             for b in range(KEY_BANKS):
                 if is_tile(step):
                     mask_scores(step, b)
@@ -373,20 +405,13 @@ def tile_spatialprocessor_pa_kernel(
                     scores(step + 1, b)
                 if is_tile(step - 1) and b < 2:
                     regroup(step - 1, b)
-            if is_tile(step - 4):
-                layer_norm(step - 4)
-            if step == 1:
-                quantise_values()
+            if is_tile(step - 3):
+                row_deviation(step - 3)
             if is_tile(step - 2):
-                quantise_e(step - 2)
+                add_streams(step - 2)
+            if is_tile(step - NORMALISE_LAG):
+                normalise(step - NORMALISE_LAG)
             if is_tile(step):
                 row_minimum(step)
-            if is_tile(step - 3):
-                add_streams(step - 3)
-            if is_tile(step - 2):
-                multiply_values(step - 2)
-            if step == 0:
-                for c in range(1, QUADS):
-                    transpose_queries(c)
-            if is_tile(step):
-                side_job_start(step)
+            if is_tile(step + 2):
+                side_job_start(step + 2)

from contextlib import ExitStack

import concourse.mybir as mybir
from concourse.masks import make_identity

F32 = mybir.dt.float32
BF16 = mybir.dt.bfloat16
I32 = mybir.dt.int32
U32 = mybir.dt.uint32
U8 = mybir.dt.uint8
FP8X4 = mybir.dt.float8_e4m3fn_x4
ALU = mybir.AluOpType
ACT = mybir.ActivationFunctionType
AXIS = mybir.AxisListType

P = 128
PACK = 4
K_PASS = P * PACK
NODES = 2048
D = 128
F_IN = 512
BANK = 512
ROW_TILES = NODES // P
KEY_BANKS = NODES // BANK
KEY_PASSES = NODES // K_PASS
QUAD = 4
QUADS = ROW_TILES // QUAD
LN_EPS = 1e-3
TURN_BANKS = 3
NORMALISE_LAG = 4

MASK_SHIFT = 2.0 ** -34
EXP_SCALE = 2.0 ** 34 / 128.0 ** 0.5

FLOPS = 2 * NODES * NODES * D * 2 + 2 * NODES * F_IN * D


def tile_spatialprocessor_pa_kernel(
    tc, q2, k2, v2, adj, x, proj_w_words, proj_w_scales, ln_g, ln_b, out
):
    nc = tc.nc
    with ExitStack() as pools:
        keep = pools.enter_context(tc.tile_pool(name="keep", bufs=1))
        adj_pool = pools.enter_context(tc.tile_pool(name="adj", bufs=ROW_TILES))
        x_pool = pools.enter_context(tc.tile_pool(name="x", bufs=QUADS))
        work = pools.enter_context(tc.tile_pool(name="work", bufs=3))
        small = pools.enter_context(tc.tile_pool(name="small", bufs=4))
        psum = pools.enter_context(tc.psum_pool(name="psum", bufs=1))
        pools.enter_context(tc.manual_schedule())

        k_rows = k2[0].rearrange("(c p m) d -> c p m d", p=P, m=PACK)
        v_rows = v2[0].rearrange("(g p t) d -> p g t d", p=P, t=PACK)
        q_rows = q2[0].rearrange("(p n) d -> p n d", n=ROW_TILES)
        adj_rows = adj.rearrange("(p n) j -> p n j", n=ROW_TILES)
        x_rows = x[0].rearrange("(p n) k -> p n k", n=ROW_TILES)
        out_rows = out[0].rearrange("(p n) d -> p n d", n=ROW_TILES)

        k_raw = keep.tile([P, KEY_BANKS, PACK, D], BF16)
        q_raw = keep.tile([P, ROW_TILES, D], BF16)
        v_raw = keep.tile([P, KEY_PASSES, PACK, D], BF16)
        kT = keep.tile([P, NODES], BF16)
        qT = keep.tile([P, ROW_TILES * P], BF16)
        v_grouped = keep.tile([P, KEY_PASSES, D, PACK], BF16, align_bytes=64)
        v_codes = keep.tile([P, KEY_PASSES * D], U32, align_bytes=64)
        v_scales = keep.tile([P, KEY_PASSES * D], U8, align_bytes=64)
        w_codes = keep.tile([P, D], U32, align_bytes=64)
        w_scales = keep.tile([P, D], U8, align_bytes=64)
        x_codes = keep.tile([P, ROW_TILES * P], U32, align_bytes=64)
        x_scales = keep.tile([P, ROW_TILES * P], U8, align_bytes=64)
        skip = keep.tile([P, ROW_TILES, D], F32)
        gain = keep.tile([P, D], BF16)
        shift = keep.tile([P, D], BF16)
        ident_bf = keep.tile([P, P], BF16)
        ident_f32 = keep.tile([P, P], F32)
        minus_one = keep.tile([P, 1], F32)
        minus_half = keep.tile([P, 1], F32)
        adj_sb = [adj_pool.tile([P, NODES], BF16, name="adj_sb") for n in range(ROW_TILES)]
        x_sb = [x_pool.tile([P, QUAD, F_IN], BF16, name="x_sb") for c in range(QUADS)]

        s_ps = {}
        t = {}
        t_min = {}
        exp_bias = {}
        e_words = {}
        row_inv = {}
        grouped = {}
        qT_ps = {}
        xT_ps = {}
        x_grouped = {}
        skip_ps = {}
        e_codes = {}
        e_scales = {}
        y_sum = {}
        neg_mean = {}
        inv_std = {}
        h_ps = {}
        y = {}

        make_identity(nc, ident_bf[:])
        make_identity(nc, ident_f32[:])
        nc.gpsimd.memset(minus_one[:], -1.0)
        nc.gpsimd.memset(minus_half[:], -0.5)
        nc.vector.memset(w_scales[:].bitcast(I32), 0)

        def load_keys(c):
            nc.sync.dma_start(out=k_raw[:, c], in_=k_rows[c])

        def load_queries(c):
            tiles = slice(QUAD * c, QUAD * (c + 1))
            nc.sync.dma_start(out=q_raw[:, tiles, :], in_=q_rows[:, tiles, :])

        def load_features(c):
            nc.sync.dma_start(out=x_sb[c][:], in_=x_rows[:, QUAD * c : QUAD * (c + 1), :])

        def load_adjacency(n):
            nc.sync.dma_start(out=adj_sb[n][:], in_=adj_rows[:, n, :])

        load_keys(0)
        load_queries(0)
        for c in range(1, KEY_BANKS):
            load_keys(c)
        load_adjacency(0)
        nc.sync.dma_start(out=v_raw[:], in_=v_rows)
        load_features(0)
        load_adjacency(1)
        for c in range(1, QUADS):
            load_queries(c)
        nc.sync.dma_start(
            out=w_codes[:].bitcast(I32),
            in_=proj_w_words[0].rearrange("p n t -> p (n t)").bitcast(I32),
        )
        for quadrant in range(4):
            nc.sync.dma_start(
                out=w_scales[32 * quadrant : 32 * quadrant + 4, :].bitcast(I32),
                in_=proj_w_scales[0, 4 * quadrant : 4 * quadrant + 4, :].bitcast(I32),
            )
        nc.sync.dma_start(out=gain[:], in_=ln_g.partition_broadcast(P))
        nc.sync.dma_start(out=shift[:], in_=ln_b.partition_broadcast(P))
        for n in range(2, ROW_TILES):
            load_adjacency(n)
            if n % QUAD == 2 and n // QUAD + 1 < QUADS:
                load_features(n // QUAD + 1)

        def transpose_keys(c):
            kT_ps = psum.tile([P, PACK, P], BF16, tag="s", bufs=KEY_BANKS)
            for m in range(PACK):
                nc.tensor.transpose(kT_ps[:, m, :], k_raw[:, c, m, :], ident_bf[:])
            nc.scalar.mul(
                out=kT[:, BANK * c : BANK * (c + 1)].rearrange("d (p m) -> d p m", m=PACK),
                in_=kT_ps[:].rearrange("d m p -> d p m"),
                mul=MASK_SHIFT,
            )

        def transpose_queries(c):
            qT_ps[c] = psum.tile([P, QUAD * P], BF16, name="qT_ps", tag="turn", bufs=TURN_BANKS)
            for m in range(QUAD):
                nc.tensor.transpose(
                    qT_ps[c][:, P * m : P * (m + 1)], q_raw[:, QUAD * c + m, :], ident_bf[:]
                )

        def keep_queries(c):
            nc.scalar.copy(out=qT[:, QUAD * P * c : QUAD * P * (c + 1)], in_=qT_ps[c][:])

        def regroup_values():
            nc.scalar.copy(out=v_grouped[:], in_=v_raw[:].rearrange("p g t d -> p g d t"))

        def quantise_values():
            nc.vector.quantize_mx(
                out=v_codes[:].bitcast(FP8X4),
                scales=v_scales[:],
                in_=v_grouped[:].rearrange("p g d t -> p (g d t)"),
            )

        def transpose_features(c, half):
            x_words = x_sb[c][:].bitcast(F32)
            xT_ps[c, half] = psum.tile([P, 2, 2, P], F32, name="xT_ps", tag="turn", bufs=TURN_BANKS)
            for m in range(2):
                for u in range(2):
                    nc.tensor.transpose(
                        xT_ps[c, half][:, m, u, :], x_words[:, 2 * half + m, u : F_IN // 2 : 2], ident_f32[:]
                    )

        def regroup_features(c, half):
            if half == 0:
                x_grouped[c] = work.tile([P, QUAD, P, PACK], BF16, name="x_grouped", align_bytes=64)
            x_grouped_words = x_grouped[c][:].bitcast(F32)
            nc.scalar.copy(
                out=x_grouped_words[:, 2 * half : 2 * half + 2, :, :],
                in_=xT_ps[c, half][:].rearrange("p m u i -> p m i u"),
            )

        def skip_product(c):
            cols = slice(QUAD * P * c, QUAD * P * (c + 1))
            nc.vector.quantize_mx(
                out=x_codes[:, cols].bitcast(FP8X4),
                scales=x_scales[:, cols],
                in_=x_grouped[c][:].rearrange("p m i t -> p (m i t)"),
            )
            skip_ps[c] = psum.tile([P, QUAD, D], F32, name="skip_ps", tag="turn", bufs=TURN_BANKS)
            for m in range(QUAD):
                nodes = slice(P * (QUAD * c + m), P * (QUAD * c + m + 1))
                nc.tensor.matmul_mx(
                    out=skip_ps[c][:, m, :],
                    lhsT=x_codes[:, nodes].bitcast(FP8X4),
                    lhsT_scale=x_scales[:, nodes],
                    rhs=w_codes[:].bitcast(FP8X4),
                    rhs_scale=w_scales[:],
                    start=True,
                    stop=True,
                )

        def keep_skip(c):
            nc.scalar.copy(out=skip[:, QUAD * c : QUAD * (c + 1), :], in_=skip_ps[c][:])

        def scores(n, b):
            s_ps[n, b] = psum.tile([P, BANK], F32, name="s_ps", tag="s", bufs=KEY_BANKS)
            nc.tensor.matmul(
                out=s_ps[n, b][:],
                lhsT=qT[:, P * n : P * (n + 1)],
                rhs=kT[:, BANK * b : BANK * (b + 1)],
                start=True,
                stop=True,
            )

        def mask_scores(n, b):
            if b == 0:
                t[n] = work.tile([P, NODES], F32, name="t")
            keys = slice(BANK * b, BANK * (b + 1))
            nc.vector.scalar_tensor_tensor(
                out=t[n][:, keys],
                in0=adj_sb[n][:, keys],
                scalar=0.0,
                in1=s_ps[n, b][:],
                op0=ALU.is_equal,
                op1=ALU.subtract,
            )

        def row_minimum(n):
            t_min[n] = small.tile([P, 1], F32, name="t_min")
            nc.vector.tensor_reduce(out=t_min[n][:], in_=t[n][:], axis=AXIS.X, op=ALU.min)

        def exponent_offset(n):
            exp_bias[n] = small.tile([P, 1], F32, name="exp_bias")
            nc.scalar.mul(out=exp_bias[n][:], in_=t_min[n][:], mul=EXP_SCALE)

        def exponentials(n):
            e_sb = work.tile([P, NODES], BF16)
            e_words[n] = e_sb[:].bitcast(F32)
            row_sums = small.tile([P, 2], F32)
            for half in range(2):
                keys = slice(NODES // 2 * half, NODES // 2 * (half + 1))
                nc.scalar.activation(
                    out=e_sb[:, keys].rearrange("i (u w e) -> i u w e", u=2, e=2),
                    in_=t[n][:, keys].rearrange("i (w u e) -> i u w e", u=2, e=2),
                    func=ACT.Exp,
                    bias=exp_bias[n][:, 0:1],
                    scale=-EXP_SCALE,
                    accum_out=row_sums[:, half : half + 1],
                )
            row_sum = small.tile([P, 1], F32)
            nc.gpsimd.tensor_tensor(out=row_sum[:], in0=row_sums[:, 0:1], in1=row_sums[:, 1:2], op=ALU.add)
            row_inv[n] = small.tile([P, 1], F32, name="row_inv")
            nc.gpsimd.tensor_tensor(out=row_inv[n][:], in0=row_sum[:], in1=minus_one[:], op=ALU.pow)

        def regroup(n, half):
            if half == 0:
                grouped[n] = work.tile([P, KEY_PASSES, P, PACK], BF16, name="grouped", align_bytes=64)
            grouped_words = grouped[n][:].bitcast(F32)
            eT_ps = psum.tile([P, 2, 2, P], F32, tag="turn", bufs=TURN_BANKS)
            for g in range(2):
                for u in range(2):
                    first = P * (4 * half + 2 * u + g)
                    nc.tensor.transpose(eT_ps[:, g, u, :], e_words[n][:, first : first + P], ident_f32[:])
            nc.scalar.copy(
                out=grouped_words[:, 2 * half : 2 * half + 2, :, :],
                in_=eT_ps[:].rearrange("p g u i -> p g i u"),
            )

        def quantise_e(n):
            e_codes[n] = work.tile([P, KEY_PASSES * P], U32, name="e_codes", align_bytes=64)
            e_scales[n] = work.tile([P, KEY_PASSES * P], U8, name="e_scales", align_bytes=64)
            for half in range(2):
                cols = slice(2 * P * half, 2 * P * (half + 1))
                nc.vector.quantize_mx(
                    out=e_codes[n][:, cols].bitcast(FP8X4),
                    scales=e_scales[n][:, cols],
                    in_=grouped[n][:, 2 * half : 2 * half + 2].rearrange("p g i t -> p (g i t)"),
                )

        def multiply_values(n):
            h_ps[n] = psum.tile([P, D], F32, name="h_ps", tag="h", bufs=1)
            for g in range(KEY_PASSES):
                cols = slice(P * g, P * (g + 1))
                nc.tensor.matmul_mx(
                    out=h_ps[n][:],
                    lhsT=e_codes[n][:, cols].bitcast(FP8X4),
                    lhsT_scale=e_scales[n][:, cols],
                    rhs=v_codes[:, cols].bitcast(FP8X4),
                    rhs_scale=v_scales[:, cols],
                    start=(g == 0),
                    stop=(g == KEY_PASSES - 1),
                )

        def add_streams(n):
            y[n] = work.tile([P, D], F32, name="y")
            y_sum[n] = small.tile([P, 1], F32, name="y_sum")
            nc.vector.scalar_tensor_tensor(
                out=y[n][:],
                in0=h_ps[n][:],
                scalar=row_inv[n][:, 0:1],
                in1=skip[:, n, :],
                op0=ALU.mult,
                op1=ALU.add,
                accum_out=y_sum[n][:],
            )

        def row_mean(n):
            neg_mean[n] = small.tile([P, 1], F32, name="neg_mean")
            nc.scalar.mul(out=neg_mean[n][:], in_=y_sum[n][:], mul=-1.0 / D)

        def row_deviation(n):
            squares = work.tile([P, D], F32)
            sq_sum = small.tile([P, 1], F32)
            nc.scalar.activation(
                out=squares[:],
                in_=y[n][:],
                func=ACT.Square,
                bias=neg_mean[n][:, 0:1],
                scale=1.0,
                accum_out=sq_sum[:],
            )
            var_eps = small.tile([P, 1], F32)
            nc.scalar.activation(out=var_eps[:], in_=sq_sum[:], func=ACT.Copy, bias=LN_EPS, scale=1.0 / D)
            inv_std[n] = small.tile([P, 1], F32, name="inv_std")
            nc.gpsimd.tensor_tensor(out=inv_std[n][:], in0=var_eps[:], in1=minus_half[:], op=ALU.pow)

        def normalise(n):
            elementwise = nc.vector if n + NORMALISE_LAG >= ROW_TILES else nc.gpsimd
            normed = work.tile([P, D], F32)
            elementwise.tensor_scalar(
                out=normed[:],
                in0=y[n][:],
                scalar1=neg_mean[n][:, 0:1],
                scalar2=inv_std[n][:, 0:1],
                op0=ALU.add,
                op1=ALU.mult,
            )
            scaled = work.tile([P, D], F32)
            elementwise.tensor_tensor(out=scaled[:], in0=normed[:], in1=gain[:], op=ALU.mult)
            result = work.tile([P, D], F32)
            elementwise.tensor_tensor(out=result[:], in0=scaled[:], in1=shift[:], op=ALU.add)
            nc.sync.dma_start(out=out_rows[:, n, :], in_=result[:])

        def is_tile(n):
            return 0 <= n < ROW_TILES

        def side_job_start(k):
            quad, phase = divmod(k, QUAD)
            if phase < 2:
                transpose_features(quad, phase)
            elif phase == 2:
                skip_product(quad)
            elif quad + 1 < QUADS:
                transpose_queries(quad + 1)

        def side_job_finish(k):
            quad, phase = divmod(k, QUAD)
            if phase < 2:
                regroup_features(quad, phase)
            elif phase == 2:
                keep_skip(quad)
            elif quad + 1 < QUADS:
                keep_queries(quad + 1)

        transpose_keys(0)
        transpose_queries(0)
        keep_queries(0)
        for c in range(1, KEY_BANKS):
            transpose_keys(c)
        for b in range(KEY_BANKS):
            scores(0, b)
        regroup_values()
        side_job_start(0)
        side_job_start(1)
        side_job_finish(0)

        for step in range(ROW_TILES + NORMALISE_LAG):
            if is_tile(step - 1):
                exponent_offset(step - 1)
            if is_tile(step - 3):
                row_mean(step - 3)
            if is_tile(step - 1):
                exponentials(step - 1)
            if is_tile(step + 1):
                side_job_finish(step + 1)
            if step == 1:
                quantise_values()
            if is_tile(step - 2):
                quantise_e(step - 2)
                multiply_values(step - 2)
            for b in range(KEY_BANKS):
                if is_tile(step):
                    mask_scores(step, b)
                if is_tile(step + 1):
                    scores(step + 1, b)
                if is_tile(step - 1) and b < 2:
                    regroup(step - 1, b)
            if is_tile(step - 3):
                row_deviation(step - 3)
            if is_tile(step - 2):
                add_streams(step - 2)
            if is_tile(step - NORMALISE_LAG):
                normalise(step - NORMALISE_LAG)
            if is_tile(step):
                row_minimum(step)
            if is_tile(step + 2):
                side_job_start(step + 2)
